import numpy as np
import ml_dtypes


def mxq(x, axis, fmt="e4m3"):
    dtype, down = {"e4m3": (ml_dtypes.float8_e4m3fn, 7), "e5m2": (ml_dtypes.float8_e5m2, 14)}[fmt]
    v = np.moveaxis(np.asarray(x, np.float32).astype(ml_dtypes.bfloat16).astype(np.float64), axis, -1)
    blocks = v.reshape(v.shape[:-1] + (-1, 32))
    amax = np.abs(blocks).max(-1, keepdims=True)
    byte = np.maximum(np.where(amax > 0, np.frexp(amax)[1] - 1 + 127, 0) - down, 1)
    scale = np.exp2(byte - 127.0)
    codes = (blocks / scale).astype(np.float32).astype(dtype).astype(np.float64)
    return np.moveaxis((codes * scale).reshape(v.shape), -1, axis)


WIDE = False


def mx_kscale(k):
    if not WIDE:
        return np.ones(k)
    levels = np.array([20, -20, 10, -10, 0])
    a = np.random.permutation(np.resize(levels, k // 512 * 4)).reshape(k // 512, 4)
    idx = np.arange(k)
    return np.exp2(a[idx // 512, idx % 128 // 32])


BF16 = ml_dtypes.bfloat16


def bf(x):
    return np.asarray(x, np.float32).astype(BF16)


def f64(x):
    return np.asarray(x).astype(np.float64)


B, C, D, O = 2, 256, 4096, 512
S0 = 1
S = 2
P = D // (S * (S0 + 1))
K = S * C
T = B * P


def setup_inputs():
    s = mx_kscale(T).reshape(B, P)
    sx = np.repeat(s, S * (S0 + 1), axis=1)[:, None, :]
    x = np.random.standard_normal((B, C, D)) * sx
    weight = np.random.standard_normal((O, C, 1, S)) / C ** 0.25
    g = np.random.standard_normal((B, O, P)) * np.exp2(np.random.randint(-12, 1, (B, 1, P))) / s[:, None, :]
    return {"x": bf(x), "weight": bf(weight), "grad_out": bf(g)}


def reference(x, weight, grad_out):
    xp = f64(x).reshape(B, C, D // (S0 + 1), S0 + 1).sum(axis=-1)
    xr = xp.reshape(B, C, P, S)
    a = xr.transpose(0, 2, 3, 1).reshape(T, K)
    g = f64(grad_out).transpose(0, 2, 1).reshape(T, O)
    gw = (mxq(g, 0, "e5m2").T @ mxq(a, 0, "e4m3")) / np.sqrt(C)
    return gw.reshape(O, S, C).transpose(0, 2, 1)[:, :, None, :]

@@ -1,0 +1,137 @@
+from contextlib import ExitStack
+
+import concourse.mybir as mybir
+from concourse.masks import make_identity
+
+BF16 = mybir.dt.bfloat16
+F32 = mybir.dt.float32
+U32 = mybir.dt.uint32
+U8 = mybir.dt.uint8
+E4M3X4 = mybir.dt.float8_e4m3fn_x4
+E5M2X4 = mybir.dt.float8_e5m2_x4
+
+P = 128
+B, C, D, O = 2, 256, 4096, 512
+TOK = 1024
+PASS = 512
+N_PASS = B * TOK // PASS
+FLOPS = 2 * B * TOK * O * 2 * C
+BYTES = 2 * B * C * D + 2 * B * O * TOK + 4 * O * C * 2
+
+
+def tile_nonoverlappingconv1d_shared_kernel(tc, x, weight, grad_out, out):
+    nc = tc.nc
+    with ExitStack() as ctx:
+        const = ctx.enter_context(tc.tile_pool(name="const", bufs=1))
+        keep = ctx.enter_context(tc.tile_pool(name="keep", bufs=1))
+        tp = ctx.enter_context(tc.psum_pool(name="tp", bufs=4))
+        accp = ctx.enter_context(tc.psum_pool(name="accp", bufs=1))
+
+        x_sb = {}
+        g_sb = {}
+        for g in range(N_PASS):
+            b, half = divmod(g, 2)
+            for h in range(2):
+                x_sb[(g, h)] = keep.tile([P, 4 * PASS], BF16, name="x%d%d" % (g, h))
+                nc.sync.dma_start(
+                    out=x_sb[(g, h)][:],
+                    in_=x[b, P * h : P * (h + 1), 4 * PASS * half : 4 * PASS * (half + 1)],
+                )
+            g_sb[g] = keep.tile([P, 4, PASS], BF16, name="g%d" % g)
+            nc.sync.dma_start(
+                out=g_sb[g][:],
+                in_=grad_out[b, :, PASS * half : PASS * (half + 1)].rearrange(
+                    "(t p) n -> p t n", p=P
+                ),
+            )
+
+        ident_bf = const.tile([P, P], BF16, name="ident_bf")
+        make_identity(nc, ident_bf[:])
+        ident_f = const.tile([P, P], F32, name="ident_f")
+        make_identity(nc, ident_f[:])
+        warm_in = const.tile([P, 1], F32, name="warm_in")
+        warm_out = const.tile([P, 1], F32, name="warm_out")
+        nc.vector.memset(warm_in[:], 0.0)
+        nc.scalar.mul(warm_out[:], warm_in[:], 1.0)
+
+        acc = [accp.tile([P, 512], F32, name="acc%d" % ot) for ot in range(4)]
+
+        for g in range(N_PASS):
+            sums = {}
+            for h in range(2):
+                s = keep.tile([P, 2, 256, 2], BF16, name="s%d%d" % (g, h))
+                xs = x_sb[(g, h)][:].rearrange("c (w e k z) -> c w e k z", e=2, k=2, z=2)
+                nc.vector.tensor_tensor(
+                    out=s[:].rearrange("c e w k -> c w e k"),
+                    in0=xs[:, :, :, :, 0],
+                    in1=xs[:, :, :, :, 1],
+                    op=mybir.AluOpType.add,
+                )
+                sums[h] = s
+            xc = keep.tile([P, 512], U32, name="xc%d" % g, align_bytes=64)
+            xsc = keep.tile([P, 512], U8, name="xsc%d" % g, align_bytes=64)
+            gc = keep.tile([P, 512], U32, name="gc%d" % g, align_bytes=64)
+            gsc = keep.tile([P, 512], U8, name="gsc%d" % g, align_bytes=64)
+            gx = {}
+            for h in range(2):
+                gx[h] = keep.tile([P, 2, P, 4], BF16, name="gx%d%d" % (g, h), align_bytes=64)
+                for k in range(2):
+                    bank = tp.tile([P, 4, P], BF16, name="bx", tag="tp")
+                    for u in range(2):
+                        for e in range(2):
+                            nc.tensor.transpose(
+                                bank[:, 2 * u + e, :],
+                                sums[h][:, e, P * u : P * (u + 1), k],
+                                ident_bf[:],
+                            )
+                    nc.scalar.copy(out=gx[h][:, k], in_=bank[:].rearrange("p t c -> p c t"))
+            gg = keep.tile([P, 512, 4], BF16, name="gg%d" % g, align_bytes=64)
+            ggw = gg[:].rearrange("p o t -> p (o t)").bitcast(F32).rearrange("p (o u) -> p o u", u=2)
+            gw = g_sb[g][:].bitcast(F32)
+            for op in range(2):
+                bank = tp.tile([P, 2, 256], F32, name="bg", tag="tp")
+                for oi in range(2):
+                    for u in range(2):
+                        nc.tensor.transpose(
+                            bank[:, u, P * oi : P * (oi + 1)],
+                            gw[:, 2 * op + oi, P * u : P * (u + 1)],
+                            ident_f[:],
+                        )
+                nc.scalar.copy(
+                    out=ggw[:, 256 * op : 256 * (op + 1), :],
+                    in_=bank[:].rearrange("p u o -> p o u"),
+                )
+            for h in range(2):
+                nc.vector.quantize_mx(
+                    out=xc[:, 256 * h : 256 * (h + 1)].bitcast(E4M3X4),
+                    scales=xsc[:, 256 * h : 256 * (h + 1)],
+                    in_=gx[h][:].rearrange("p k c t -> p (k c t)"),
+                )
+            nc.vector.quantize_mx(
+                out=gc[:].bitcast(E5M2X4),
+                scales=gsc[:],
+                in_=gg[:].rearrange("p o t -> p (o t)"),
+            )
+            for ot in range(4):
+                nc.tensor.matmul_mx(
+                    out=acc[ot][:],
+                    lhsT=gc[:, P * ot : P * (ot + 1)].bitcast(E5M2X4),
+                    lhsT_scale=gsc[:, P * ot : P * (ot + 1)],
+                    rhs=xc[:].bitcast(E4M3X4),
+                    rhs_scale=xsc[:],
+                    start=(g == 0),
+                    stop=(g == N_PASS - 1),
+                )
+
+        for ot in range(4):
+            res = keep.tile([P, 512], F32, name="res%d" % ot)
+            src = acc[ot][:].rearrange("o (h k c) -> o h c k", h=2, k=2)
+            dst = res[:].rearrange("o (h c k) -> o h c k", h=2, k=2)
+            if ot % 2 == 0:
+                nc.vector.tensor_scalar_mul(dst, src, 0.0625)
+            else:
+                nc.scalar.mul(dst, src, 0.0625)
+            nc.sync.dma_start(
+                out=out[P * ot : P * (ot + 1)].rearrange("o c one k -> o (c one k)"),
+                in_=res[:],
+            )

@@ -18,32 +18,46 @@ N_PASS = B * TOK // PASS
 FLOPS = 2 * B * TOK * O * 2 * C
 BYTES = 2 * B * C * D + 2 * B * O * TOK + 4 * O * C * 2
 
+N_X = 8
+N_Y = 8
+Y_LAG = 2
+Q_LAG = 2
+MIN_BUNCH = 4
+FLUSH_FROM = 9
+N_SLOT = 14
+
 
 def tile_nonoverlappingconv1d_shared_kernel(tc, x, weight, grad_out, out):
     nc = tc.nc
     with ExitStack() as ctx:
+        ctx.enter_context(tc.manual_schedule())
         const = ctx.enter_context(tc.tile_pool(name="const", bufs=1))
         keep = ctx.enter_context(tc.tile_pool(name="keep", bufs=1))
         tp = ctx.enter_context(tc.psum_pool(name="tp", bufs=4))
         accp = ctx.enter_context(tc.psum_pool(name="accp", bufs=1))
 
-        x_sb = {}
-        g_sb = {}
-        for g in range(N_PASS):
+        x_sb = [keep.tile([P, 4 * PASS], BF16, name="x%d" % i) for i in range(N_X)]
+        y_sb = [keep.tile([P, TOK], BF16, name="y%d" % j) for j in range(N_Y)]
+
+        def load_x(i, lo, hi):
+            g, h = divmod(i, 2)
             b, half = divmod(g, 2)
-            for h in range(2):
-                x_sb[(g, h)] = keep.tile([P, 4 * PASS], BF16, name="x%d%d" % (g, h))
-                nc.sync.dma_start(
-                    out=x_sb[(g, h)][:],
-                    in_=x[b, P * h : P * (h + 1), 4 * PASS * half : 4 * PASS * (half + 1)],
-                )
-            g_sb[g] = keep.tile([P, 4, PASS], BF16, name="g%d" % g)
             nc.sync.dma_start(
-                out=g_sb[g][:],
-                in_=grad_out[b, :, PASS * half : PASS * (half + 1)].rearrange(
-                    "(t p) n -> p t n", p=P
-                ),
+                out=x_sb[i][:, lo:hi],
+                in_=x[b, P * h : P * (h + 1), 4 * PASS * half + lo : 4 * PASS * half + hi],
             )
+
+        def load_y(j):
+            b, ot = divmod(j, 4)
+            nc.sync.dma_start(out=y_sb[j][:], in_=grad_out[b, P * ot : P * (ot + 1), :])
+
+        load_x(0, 0, 2 * PASS)
+        load_x(0, 2 * PASS, 4 * PASS)
+        for s in range(1, N_SLOT):
+            if s < N_X:
+                load_x(s, 0, 4 * PASS)
+            if 0 <= s - Y_LAG < N_Y:
+                load_y(s - Y_LAG)
 
         ident_bf = const.tile([P, P], BF16, name="ident_bf")
         make_identity(nc, ident_bf[:])
@@ -55,73 +69,121 @@ def tile_nonoverlappingconv1d_shared_kernel(tc, x, weight, grad_out, out):
         nc.scalar.mul(warm_out[:], warm_in[:], 1.0)
 
         acc = [accp.tile([P, 512], F32, name="acc%d" % ot) for ot in range(4)]
+        sums = [keep.tile([P, 2, 256, 2], BF16, name="s%d" % i) for i in range(N_X)]
+        gx = [keep.tile([P, 2, P, 4], BF16, name="gx%d" % i, align_bytes=64) for i in range(N_X)]
+        gy = [keep.tile([P, 2, P, 4], BF16, name="gy%d" % j, align_bytes=64) for j in range(N_Y)]
+        xc = [keep.tile([P, 512], U32, name="xc%d" % g, align_bytes=64) for g in range(N_PASS)]
+        xs = [keep.tile([P, 512], U8, name="xs%d" % g, align_bytes=64) for g in range(N_PASS)]
+        yc = [keep.tile([P, 256], U32, name="yc%d" % j, align_bytes=64) for j in range(N_Y)]
+        ys = [keep.tile([P, 256], U8, name="ys%d" % j, align_bytes=64) for j in range(N_Y)]
 
-        for g in range(N_PASS):
-            sums = {}
-            for h in range(2):
-                s = keep.tile([P, 2, 256, 2], BF16, name="s%d%d" % (g, h))
-                xs = x_sb[(g, h)][:].rearrange("c (w e k z) -> c w e k z", e=2, k=2, z=2)
-                nc.vector.tensor_tensor(
-                    out=s[:].rearrange("c e w k -> c w e k"),
-                    in0=xs[:, :, :, :, 0],
-                    in1=xs[:, :, :, :, 1],
-                    op=mybir.AluOpType.add,
-                )
-                sums[h] = s
-            xc = keep.tile([P, 512], U32, name="xc%d" % g, align_bytes=64)
-            xsc = keep.tile([P, 512], U8, name="xsc%d" % g, align_bytes=64)
-            gc = keep.tile([P, 512], U32, name="gc%d" % g, align_bytes=64)
-            gsc = keep.tile([P, 512], U8, name="gsc%d" % g, align_bytes=64)
-            gx = {}
-            for h in range(2):
-                gx[h] = keep.tile([P, 2, P, 4], BF16, name="gx%d%d" % (g, h), align_bytes=64)
-                for k in range(2):
-                    bank = tp.tile([P, 4, P], BF16, name="bx", tag="tp")
-                    for u in range(2):
-                        for e in range(2):
-                            nc.tensor.transpose(
-                                bank[:, 2 * u + e, :],
-                                sums[h][:, e, P * u : P * (u + 1), k],
-                                ident_bf[:],
-                            )
-                    nc.scalar.copy(out=gx[h][:, k], in_=bank[:].rearrange("p t c -> p c t"))
-            gg = keep.tile([P, 512, 4], BF16, name="gg%d" % g, align_bytes=64)
-            ggw = gg[:].rearrange("p o t -> p (o t)").bitcast(F32).rearrange("p (o u) -> p o u", u=2)
-            gw = g_sb[g][:].bitcast(F32)
-            for op in range(2):
-                bank = tp.tile([P, 2, 256], F32, name="bg", tag="tp")
-                for oi in range(2):
-                    for u in range(2):
-                        nc.tensor.transpose(
-                            bank[:, u, P * oi : P * (oi + 1)],
-                            gw[:, 2 * op + oi, P * u : P * (u + 1)],
-                            ident_f[:],
-                        )
-                nc.scalar.copy(
-                    out=ggw[:, 256 * op : 256 * (op + 1), :],
-                    in_=bank[:].rearrange("p u o -> p o u"),
-                )
-            for h in range(2):
-                nc.vector.quantize_mx(
-                    out=xc[:, 256 * h : 256 * (h + 1)].bitcast(E4M3X4),
-                    scales=xsc[:, 256 * h : 256 * (h + 1)],
-                    in_=gx[h][:].rearrange("p k c t -> p (k c t)"),
-                )
-            nc.vector.quantize_mx(
-                out=gc[:].bitcast(E5M2X4),
-                scales=gsc[:],
-                in_=gg[:].rearrange("p o t -> p (o t)"),
+        def add_x(i, u0, u1):
+            src = x_sb[i][:, 1024 * u0 : 1024 * u1].rearrange(
+                "c (w e k z) -> c w e k z", e=2, k=2, z=2
             )
-            for ot in range(4):
-                nc.tensor.matmul_mx(
-                    out=acc[ot][:],
-                    lhsT=gc[:, P * ot : P * (ot + 1)].bitcast(E5M2X4),
-                    lhsT_scale=gsc[:, P * ot : P * (ot + 1)],
-                    rhs=xc[:].bitcast(E4M3X4),
-                    rhs_scale=xsc[:],
-                    start=(g == 0),
-                    stop=(g == N_PASS - 1),
-                )
+            nc.vector.tensor_tensor(
+                out=sums[i][:, :, P * u0 : P * u1, :].rearrange("c e w k -> c w e k"),
+                in0=src[:, :, :, :, 0],
+                in1=src[:, :, :, :, 1],
+                op=mybir.AluOpType.add,
+            )
+
+        def transpose_x(i, k):
+            bank = tp.tile([P, 4, P], BF16, name="bx", tag="tp")
+            for u in range(2):
+                for e in range(2):
+                    nc.tensor.transpose(
+                        bank[:, 2 * u + e, :], sums[i][:, e, P * u : P * (u + 1), k], ident_bf[:]
+                    )
+            return bank
+
+        def exit_x(i, k, bank):
+            nc.scalar.copy(out=gx[i][:, k], in_=bank[:].rearrange("p t c -> p c t"))
+
+        def quant_x(i):
+            g, h = divmod(i, 2)
+            nc.vector.quantize_mx(
+                out=xc[g][:, 256 * h : 256 * (h + 1)].bitcast(E4M3X4),
+                scales=xs[g][:, 256 * h : 256 * (h + 1)],
+                in_=gx[i][:].rearrange("p k c t -> p (k c t)"),
+            )
+
+        def transpose_y(j):
+            words = y_sb[j][:].bitcast(F32)
+            bank = tp.tile([P, 2, 2, P], F32, name="by", tag="tp")
+            for half in range(2):
+                for u in range(2):
+                    nc.tensor.transpose(
+                        bank[:, half, u, :],
+                        words[:, 256 * half + P * u : 256 * half + P * (u + 1)],
+                        ident_f[:],
+                    )
+            return bank
+
+        def exit_y(j, bank):
+            dst = gy[j][:].rearrange("p a o t -> p (a o t)").bitcast(F32)
+            nc.scalar.copy(
+                out=dst.rearrange("p (a o u) -> p a o u", a=2, u=2),
+                in_=bank[:].rearrange("p a u o -> p a o u"),
+            )
+
+        def quant_y(j):
+            nc.vector.quantize_mx(
+                out=yc[j][:].bitcast(E5M2X4),
+                scales=ys[j][:],
+                in_=gy[j][:].rearrange("p a o t -> p (a o t)"),
+            )
+
+        def mx(g, ot):
+            b, half = divmod(g, 2)
+            j = 4 * b + ot
+            nc.tensor.matmul_mx(
+                out=acc[ot][:],
+                lhsT=yc[j][:, P * half : P * (half + 1)].bitcast(E5M2X4),
+                lhsT_scale=ys[j][:, P * half : P * (half + 1)],
+                rhs=xc[g][:].bitcast(E4M3X4),
+                rhs_scale=xs[g][:],
+                start=(g == 0),
+                stop=(g == N_PASS - 1),
+            )
+
+        quantised = set()
+        issued = set()
+        for s in range(N_SLOT):
+            if s == 0:
+                add_x(0, 0, 1)
+                add_x(0, 1, 2)
+            elif s < N_X:
+                add_x(s, 0, 2)
+            if 0 <= s - Q_LAG < N_X:
+                quant_x(s - Q_LAG)
+                quantised.add(("x", s - Q_LAG))
+            if 0 <= s - Y_LAG - Q_LAG < N_Y:
+                quant_y(s - Y_LAG - Q_LAG)
+                quantised.add(("y", s - Y_LAG - Q_LAG))
+            if 0 <= s - Y_LAG < N_Y:
+                exit_y(s - Y_LAG, transpose_y(s - Y_LAG))
+            if s < N_X:
+                banks = [transpose_x(s, k) for k in range(2)]
+                for k in range(2):
+                    exit_x(s, k, banks[k])
+            ready = []
+            for g in range(N_PASS):
+                for ot in range(4):
+                    if (g, ot) in issued:
+                        continue
+                    have = (
+                        ("x", 2 * g) in quantised
+                        and ("x", 2 * g + 1) in quantised
+                        and ("y", 4 * (g // 2) + ot) in quantised
+                    )
+                    before = g == 0 or (g - 1, ot) in issued or (g - 1, ot) in ready
+                    if have and before:
+                        ready.append((g, ot))
+            if len(ready) >= MIN_BUNCH or s >= FLUSH_FROM:
+                for g, ot in ready:
+                    mx(g, ot)
+                    issued.add((g, ot))
 
         for ot in range(4):
             res = keep.tile([P, 512], F32, name="res%d" % ot)

@@ -25,6 +25,9 @@ Q_LAG = 2
 MIN_BUNCH = 4
 FLUSH_FROM = 9
 N_SLOT = 14
+WARM_FIRST = 4
+WARM_SLOT = 2
+WARM_SLOTS = 4
 
 
 def tile_nonoverlappingconv1d_shared_kernel(tc, x, weight, grad_out, out):
@@ -147,6 +150,16 @@ def tile_nonoverlappingconv1d_shared_kernel(tc, x, weight, grad_out, out):
                 stop=(g == N_PASS - 1),
             )
 
+        def keep_clock(n):
+            for r in range(n):
+                nc.tensor.matmul(
+                    out=acc[3][:, 0:256],
+                    lhsT=ident_bf[:],
+                    rhs=x_sb[0][:, 0:256],
+                    start=True,
+                    stop=True,
+                )
+
         quantised = set()
         issued = set()
         for s in range(N_SLOT):
@@ -163,6 +176,10 @@ def tile_nonoverlappingconv1d_shared_kernel(tc, x, weight, grad_out, out):
                 quantised.add(("y", s - Y_LAG - Q_LAG))
             if 0 <= s - Y_LAG < N_Y:
                 exit_y(s - Y_LAG, transpose_y(s - Y_LAG))
+            if s == 0:
+                keep_clock(WARM_FIRST)
+            elif s <= WARM_SLOTS:
+                keep_clock(WARM_SLOT)
             if s < N_X:
                 banks = [transpose_x(s, k) for k in range(2)]
                 for k in range(2):

from contextlib import ExitStack

import concourse.mybir as mybir
from concourse.masks import make_identity

BF16 = mybir.dt.bfloat16
F32 = mybir.dt.float32
U32 = mybir.dt.uint32
U8 = mybir.dt.uint8
E4M3X4 = mybir.dt.float8_e4m3fn_x4
E5M2X4 = mybir.dt.float8_e5m2_x4

P = 128
B, C, D, O = 2, 256, 4096, 512
TOK = 1024
PASS = 512
N_PASS = B * TOK // PASS
FLOPS = 2 * B * TOK * O * 2 * C
BYTES = 2 * B * C * D + 2 * B * O * TOK + 4 * O * C * 2

N_X = 8
N_Y = 8
Y_LAG = 2
Q_LAG = 2
MIN_BUNCH = 4
FLUSH_FROM = 9
N_SLOT = 14
WARM_FIRST = 4
WARM_SLOT = 2
WARM_SLOTS = 4


def tile_nonoverlappingconv1d_shared_kernel(tc, x, weight, grad_out, out):
    nc = tc.nc
    with ExitStack() as ctx:
        ctx.enter_context(tc.manual_schedule())
        const = ctx.enter_context(tc.tile_pool(name="const", bufs=1))
        keep = ctx.enter_context(tc.tile_pool(name="keep", bufs=1))
        tp = ctx.enter_context(tc.psum_pool(name="tp", bufs=4))
        accp = ctx.enter_context(tc.psum_pool(name="accp", bufs=1))

        x_sb = [keep.tile([P, 4 * PASS], BF16, name="x%d" % i) for i in range(N_X)]
        y_sb = [keep.tile([P, TOK], BF16, name="y%d" % j) for j in range(N_Y)]

        def load_x(i, lo, hi):
            g, h = divmod(i, 2)
            b, half = divmod(g, 2)
            nc.sync.dma_start(
                out=x_sb[i][:, lo:hi],
                in_=x[b, P * h : P * (h + 1), 4 * PASS * half + lo : 4 * PASS * half + hi],
            )

        def load_y(j):
            b, ot = divmod(j, 4)
            nc.sync.dma_start(out=y_sb[j][:], in_=grad_out[b, P * ot : P * (ot + 1), :])

        load_x(0, 0, 2 * PASS)
        load_x(0, 2 * PASS, 4 * PASS)
        for s in range(1, N_SLOT):
            if s < N_X:
                load_x(s, 0, 4 * PASS)
            if 0 <= s - Y_LAG < N_Y:
                load_y(s - Y_LAG)

        ident_bf = const.tile([P, P], BF16, name="ident_bf")
        make_identity(nc, ident_bf[:])
        ident_f = const.tile([P, P], F32, name="ident_f")
        make_identity(nc, ident_f[:])
        warm_in = const.tile([P, 1], F32, name="warm_in")
        warm_out = const.tile([P, 1], F32, name="warm_out")
        nc.vector.memset(warm_in[:], 0.0)
        nc.scalar.mul(warm_out[:], warm_in[:], 1.0)

        acc = [accp.tile([P, 512], F32, name="acc%d" % ot) for ot in range(4)]
        sums = [keep.tile([P, 2, 256, 2], BF16, name="s%d" % i) for i in range(N_X)]
        gx = [keep.tile([P, 2, P, 4], BF16, name="gx%d" % i, align_bytes=64) for i in range(N_X)]
        gy = [keep.tile([P, 2, P, 4], BF16, name="gy%d" % j, align_bytes=64) for j in range(N_Y)]
        xc = [keep.tile([P, 512], U32, name="xc%d" % g, align_bytes=64) for g in range(N_PASS)]
        xs = [keep.tile([P, 512], U8, name="xs%d" % g, align_bytes=64) for g in range(N_PASS)]
        yc = [keep.tile([P, 256], U32, name="yc%d" % j, align_bytes=64) for j in range(N_Y)]
        ys = [keep.tile([P, 256], U8, name="ys%d" % j, align_bytes=64) for j in range(N_Y)]

        def add_x(i, u0, u1):
            src = x_sb[i][:, 1024 * u0 : 1024 * u1].rearrange(
                "c (w e k z) -> c w e k z", e=2, k=2, z=2
            )
            nc.vector.tensor_tensor(
                out=sums[i][:, :, P * u0 : P * u1, :].rearrange("c e w k -> c w e k"),
                in0=src[:, :, :, :, 0],
                in1=src[:, :, :, :, 1],
                op=mybir.AluOpType.add,
            )

        def transpose_x(i, k):
            bank = tp.tile([P, 4, P], BF16, name="bx", tag="tp")
            for u in range(2):
                for e in range(2):
                    nc.tensor.transpose(
                        bank[:, 2 * u + e, :], sums[i][:, e, P * u : P * (u + 1), k], ident_bf[:]
                    )
            return bank

        def exit_x(i, k, bank):
            nc.scalar.copy(out=gx[i][:, k], in_=bank[:].rearrange("p t c -> p c t"))

        def quant_x(i):
            g, h = divmod(i, 2)
            nc.vector.quantize_mx(
                out=xc[g][:, 256 * h : 256 * (h + 1)].bitcast(E4M3X4),
                scales=xs[g][:, 256 * h : 256 * (h + 1)],
                in_=gx[i][:].rearrange("p k c t -> p (k c t)"),
            )

        def transpose_y(j):
            words = y_sb[j][:].bitcast(F32)
            bank = tp.tile([P, 2, 2, P], F32, name="by", tag="tp")
            for half in range(2):
                for u in range(2):
                    nc.tensor.transpose(
                        bank[:, half, u, :],
                        words[:, 256 * half + P * u : 256 * half + P * (u + 1)],
                        ident_f[:],
                    )
            return bank

        def exit_y(j, bank):
            dst = gy[j][:].rearrange("p a o t -> p (a o t)").bitcast(F32)
            nc.scalar.copy(
                out=dst.rearrange("p (a o u) -> p a o u", a=2, u=2),
                in_=bank[:].rearrange("p a u o -> p a o u"),
            )

        def quant_y(j):
            nc.vector.quantize_mx(
                out=yc[j][:].bitcast(E5M2X4),
                scales=ys[j][:],
                in_=gy[j][:].rearrange("p a o t -> p (a o t)"),
            )

        def mx(g, ot):
            b, half = divmod(g, 2)
            j = 4 * b + ot
            nc.tensor.matmul_mx(
                out=acc[ot][:],
                lhsT=yc[j][:, P * half : P * (half + 1)].bitcast(E5M2X4),
                lhsT_scale=ys[j][:, P * half : P * (half + 1)],
                rhs=xc[g][:].bitcast(E4M3X4),
                rhs_scale=xs[g][:],
                start=(g == 0),
                stop=(g == N_PASS - 1),
            )

        def keep_clock(n):
            for r in range(n):
                nc.tensor.matmul(
                    out=acc[3][:, 0:256],
                    lhsT=ident_bf[:],
                    rhs=x_sb[0][:, 0:256],
                    start=True,
                    stop=True,
                )

        quantised = set()
        issued = set()
        for s in range(N_SLOT):
            if s == 0:
                add_x(0, 0, 1)
                add_x(0, 1, 2)
            elif s < N_X:
                add_x(s, 0, 2)
            if 0 <= s - Q_LAG < N_X:
                quant_x(s - Q_LAG)
                quantised.add(("x", s - Q_LAG))
            if 0 <= s - Y_LAG - Q_LAG < N_Y:
                quant_y(s - Y_LAG - Q_LAG)
                quantised.add(("y", s - Y_LAG - Q_LAG))
            if 0 <= s - Y_LAG < N_Y:
                exit_y(s - Y_LAG, transpose_y(s - Y_LAG))
            if s == 0:
                keep_clock(WARM_FIRST)
            elif s <= WARM_SLOTS:
                keep_clock(WARM_SLOT)
            if s < N_X:
                banks = [transpose_x(s, k) for k in range(2)]
                for k in range(2):
                    exit_x(s, k, banks[k])
            ready = []
            for g in range(N_PASS):
                for ot in range(4):
                    if (g, ot) in issued:
                        continue
                    have = (
                        ("x", 2 * g) in quantised
                        and ("x", 2 * g + 1) in quantised
                        and ("y", 4 * (g // 2) + ot) in quantised
                    )
                    before = g == 0 or (g - 1, ot) in issued or (g - 1, ot) in ready
                    if have and before:
                        ready.append((g, ot))
            if len(ready) >= MIN_BUNCH or s >= FLUSH_FROM:
                for g, ot in ready:
                    mx(g, ot)
                    issued.add((g, ot))

        for ot in range(4):
            res = keep.tile([P, 512], F32, name="res%d" % ot)
            src = acc[ot][:].rearrange("o (h k c) -> o h c k", h=2, k=2)
            dst = res[:].rearrange("o (h c k) -> o h c k", h=2, k=2)
            if ot % 2 == 0:
                nc.vector.tensor_scalar_mul(dst, src, 0.0625)
            else:
                nc.scalar.mul(dst, src, 0.0625)
            nc.sync.dma_start(
                out=out[P * ot : P * (ot + 1)].rearrange("o c one k -> o (c one k)"),
                in_=res[:],
            )
